import numpy as np
import ml_dtypes


def mxq(x, axis, fmt="e4m3"):
    dtype, down = {"e4m3": (ml_dtypes.float8_e4m3fn, 7), "e5m2": (ml_dtypes.float8_e5m2, 14)}[fmt]
    v = np.moveaxis(np.asarray(x, np.float32).astype(ml_dtypes.bfloat16).astype(np.float64), axis, -1)
    blocks = v.reshape(v.shape[:-1] + (-1, 32))
    amax = np.abs(blocks).max(-1, keepdims=True)
    byte = np.maximum(np.where(amax > 0, np.frexp(amax)[1] - 1 + 127, 0) - down, 1)
    scale = np.exp2(byte - 127.0)
    codes = (blocks / scale).astype(np.float32).astype(dtype).astype(np.float64)
    return np.moveaxis((codes * scale).reshape(v.shape), -1, axis)


WIDE = False


def mx_kscale(k):
    if not WIDE:
        return np.ones(k)
    levels = np.array([10, -10, 5, -5, 0])
    if k % 512:
        return np.exp2(np.random.permutation(np.resize(levels, k // 32))).repeat(32)
    a = np.empty((k // 512, 16))
    for p in range(k // 512):
        a[p, :8] = np.random.permutation(np.resize(levels, 8))
        for g in range(8):
            far = levels[np.abs(levels - a[p, g]) >= 10]
            a[p, g + 8] = far[np.random.randint(len(far))]
    return np.exp2(a.ravel()).repeat(32)


BF16 = ml_dtypes.bfloat16


def bf(x):
    return np.asarray(x, np.float32).astype(BF16)


def f64(x):
    return np.asarray(x).astype(np.float64)


E, D_COMM, D_REL, D_HET, D_HID = 16384, 1024, 512, 128, 512
D_IN = D_COMM + D_REL


def draw0():
    s, t = mx_kscale(D_REL), mx_kscale(D_HID)
    spread = np.exp(0.5 * np.random.standard_normal((E, 1)))
    return {"Mij": bf(np.random.standard_normal((E, D_REL)) * s),
            "f_weights": bf(np.random.standard_normal((E, D_HET)) * np.sqrt(2.0 / D_HET) * spread),
            "W1_rel": bf(np.random.standard_normal((D_REL, D_HID)) / np.sqrt(D_IN) / s[:, None] * t),
            "node_bias": bf(np.random.standard_normal(D_HID) * np.sqrt(D_COMM / D_IN) * t),
            "W2": bf(np.random.standard_normal((D_HID, D_HET)) / np.sqrt(D_HID) / t[:, None]),
            "b2": bf(np.random.standard_normal(D_HET) * 0.1)}


def core(Mij, f_weights, W1_rel, node_bias, W2, b2):
    h = np.maximum((mxq(f64(Mij), 1, "e4m3") @ mxq(f64(W1_rel), 0, "e4m3")) + f64(node_bias), 0.0)
    out = (mxq(h, 1, "e4m3") @ mxq(f64(W2), 0, "e4m3")) + f64(b2)
    msg = out * f64(f_weights)
    norm = np.sqrt((msg * msg).sum(axis=1, keepdims=True))
    scale = np.where(norm > 1.0, 1.0 / np.maximum(norm, 1.0), 1.0)
    return msg * scale


def e4m3fn_bytes(y):
    return np.clip(np.asarray(y, np.float64), -448.0, 448.0).astype(np.float32).astype(ml_dtypes.float8_e4m3fn).view(np.uint8)


def e4m3fn_values(b):
    return np.asarray(b, np.uint8).view(ml_dtypes.float8_e4m3fn).astype(np.float64)


def setup_inputs():
    d = draw0()
    x0 = np.asarray(d['Mij']).astype(np.float64)
    s = (np.max(np.abs(x0), axis=(0,), keepdims=True) / 448.0).astype(np.float32)
    out = {}
    for k, v in d.items():
        if k == 'Mij':
            out['Mij_bytes'] = e4m3fn_bytes(x0 / s.astype(np.float64))
            out['Mij_scale'] = s
        else:
            out[k] = v
    return out


def reference(Mij_bytes, Mij_scale, f_weights, W1_rel, node_bias, W2, b2):
    return core(e4m3fn_values(Mij_bytes) * Mij_scale.astype(np.float64), f_weights, W1_rel, node_bias, W2, b2)

@@ -1,0 +1,250 @@
+from contextlib import ExitStack
+
+import concourse.mybir as mybir
+from concourse.masks import make_identity
+
+E, K, H, N = 16384, 512, 512, 128
+P = 128
+TOK = 512
+J = TOK // P
+STEPS = E // TOK
+FLOPS = 2 * E * H * (K + N)
+
+F32 = mybir.dt.float32
+BF16 = mybir.dt.bfloat16
+U32 = mybir.dt.uint32
+U8 = mybir.dt.uint8
+FP8 = mybir.dt.float8_e4m3fn
+FP8X4 = mybir.dt.float8_e4m3fn_x4
+ACT = mybir.ActivationFunctionType
+ALU = mybir.AluOpType
+
+
+def tile_filter_pa_t_kernel(tc, x_bytes, x_scale, f_weights, w1, node_bias, w2, b2, out):
+    nc = tc.nc
+    x_view = x_bytes.rearrange("(g p j) k -> g p (j k)", p=P, j=J)
+    f_view = f_weights.rearrange("(g p j) n -> g p (j n)", p=P, j=J)
+    o_view = out.rearrange("(g p j) n -> g p (j n)", p=P, j=J)
+
+    with ExitStack() as ctx:
+        const = ctx.enter_context(tc.tile_pool(name="const", bufs=1))
+        load = ctx.enter_context(tc.tile_pool(name="load", bufs=5))
+        fload = ctx.enter_context(tc.tile_pool(name="fload", bufs=9))
+        one = ctx.enter_context(tc.tile_pool(name="one", bufs=1))
+        work = ctx.enter_context(tc.tile_pool(name="work", bufs=3))
+        tail = ctx.enter_context(tc.tile_pool(name="tail", bufs=6))
+        xt_pool = ctx.enter_context(tc.psum_pool(name="xt_pool", bufs=2))
+        h_pool = ctx.enter_context(tc.psum_pool(name="h_pool", bufs=4))
+        o_pool = ctx.enter_context(tc.psum_pool(name="o_pool", bufs=2))
+        ctx.enter_context(tc.manual_schedule())
+
+        xb, fb = {}, {}
+
+        def fetch(g):
+            if g >= STEPS:
+                return
+            xb_t = load.tile([P, J * K], U8, name="xb_t", align_bytes=64)
+            nc.sync.dma_start(out=xb_t[:], in_=x_view[g])
+            xb[g] = xb_t
+            fb_t = fload.tile([P, J * N], BF16, name="fb_t", align_bytes=64)
+            nc.sync.dma_start(out=fb_t[:], in_=f_view[g])
+            fb[g] = fb_t
+
+        fetch(0)
+        sc = const.tile([P, 4], F32, name="sc", align_bytes=64)
+        nc.sync.dma_start(out=sc[:], in_=x_scale.rearrange("o (p t) -> p (o t)", t=4))
+        w1_raw = const.tile([P, 4, H], BF16, name="w1_raw", align_bytes=64)
+        nc.sync.dma_start(out=w1_raw[:], in_=w1.rearrange("(p j) c -> p j c", j=4))
+        nb_raw = const.tile([P, 4], BF16, name="nb_raw")
+        nc.sync.dma_start(out=nb_raw[:], in_=node_bias.rearrange("(p t) -> p t", t=4))
+        fetch(1)
+        w2_raw = const.tile([P, 4, N], BF16, name="w2_raw", align_bytes=64)
+        nc.sync.dma_start(out=w2_raw[:], in_=w2.rearrange("(p j) n -> p j n", j=4))
+        b2_raw = const.tile([P, N], BF16, name="b2_raw", align_bytes=64)
+        nc.sync.dma_start(out=b2_raw[:], in_=b2.partition_broadcast(P))
+        fetch(2)
+
+        ident = const.tile([P, P], F32, name="ident", align_bytes=64)
+        make_identity(nc, ident[:])
+
+        warm = const.tile([P, 1], F32, name="warm")
+        nc.vector.memset(warm[:], 1.0)
+        warm2 = const.tile([P, 1], F32, name="warm2")
+        nc.scalar.activation(out=warm2[:], in_=warm[:], func=ACT.Sqrt)
+
+        nbias = const.tile([P, 4], F32, name="nbias")
+        w1_g = const.tile([P, 4 * H], BF16, name="w1_g", align_bytes=64)
+        w1_q = const.tile([P, H], U32, name="w1_q", align_bytes=64)
+        w1_s = const.tile([P, H], U8, name="w1_s", align_bytes=64)
+        w2_g = const.tile([P, 4 * N], BF16, name="w2_g", align_bytes=64)
+        w2_q = const.tile([P, N], U32, name="w2_q", align_bytes=64)
+        w2_s = const.tile([P, N], U8, name="w2_s", align_bytes=64)
+        b2_f = const.tile([P, J, N], F32, name="b2_f", align_bytes=64)
+
+
+        xw, xt, xg, xq, xs, ht, hp, hg, hq, hs, ot, m0, mm, ss, fac, yt = ({} for _ in range(16))
+
+        def widen(g):
+            if not 0 <= g < STEPS:
+                return
+            t = work.tile([P, J * K], BF16, name="xw_t", align_bytes=64)
+            xw[g] = t
+            nc.scalar.copy(out=t[:], in_=xb[g][:].bitcast(FP8))
+
+        def turn(g):
+            if not 0 <= g < STEPS:
+                return
+            words = xw[g][:].bitcast(F32)
+            xt[g] = []
+            for b in range(2):
+                t = xt_pool.tile([P, 2, 2 * P], F32, name="xt_t")
+                for jj in range(2):
+                    j = 2 * b + jj
+                    for u in range(2):
+                        nc.tensor.transpose(t[:, u, jj * P : (jj + 1) * P], words[:, j * (K // 2) + u : (j + 1) * (K // 2) : 2], ident[:])
+                xt[g].append(t)
+
+        def unturn(g):
+            if not 0 <= g < STEPS:
+                return
+            t = work.tile([P, TOK * 4], BF16, name="xg_t", align_bytes=64)
+            xg[g] = t
+            for b in range(2):
+                nc.vector.tensor_tensor(
+                    out=t[:, b * 1024 : (b + 1) * 1024].rearrange("p (r u e) -> p r u e", u=2, e=2),
+                    in0=xt[g][b][:].rearrange("p u r -> p (u r)").bitcast(BF16).rearrange("p (u r e) -> p r u e", u=2, e=2),
+                    in1=sc[:].rearrange("p (o u e) -> p o u e", o=1, u=2).to_broadcast([P, 2 * P, 2, 2]),
+                    op=ALU.mult,
+                )
+
+        def quant_x(g):
+            if not 0 <= g < STEPS:
+                return
+            xq[g] = work.tile([P, TOK], U32, name="xq_t", align_bytes=64)
+            xs[g] = work.tile([P, TOK], U8, name="xs_t", align_bytes=64)
+            nc.vector.quantize_mx(out=xq[g][:].bitcast(FP8X4), scales=xs[g][:], in_=xg[g][:])
+
+        def mm1(g):
+            if not 0 <= g < STEPS:
+                return
+            ht[g] = []
+            for t in range(4):
+                h = h_pool.tile([P, TOK], F32, name="h_t")
+                nc.tensor.matmul_mx(out=h[:], lhsT=w1_q[:, t * P : (t + 1) * P].bitcast(FP8X4), lhsT_scale=w1_s[:, t * P : (t + 1) * P], rhs=xq[g][:].bitcast(FP8X4), rhs_scale=xs[g][:], start=True, stop=True)
+                ht[g].append(h)
+
+        def relu(g):
+            if not 0 <= g < STEPS:
+                return
+            hp[g] = work.tile([P, 4, TOK], BF16, name="hp_t", align_bytes=64)
+            for t in range(4):
+                nc.scalar.activation(out=hp[g][:, t, :], in_=ht[g][t][:], func=ACT.Relu, bias=nbias[:, t : t + 1])
+
+        def weave_parts(g, c0, c1):
+            dst = hg[g][:, 4 * c0 : 4 * c1].rearrange("p (c i t) -> p c t i", i=4, t=4)
+            src = hp[g][:, :, c0:c1].rearrange("p t (c i) -> p c t i", i=4)
+            return dst, src
+
+        def weave(g):
+            if not 0 <= g < STEPS:
+                return
+            hg[g] = one.tile([P, TOK * 4], BF16, name="hg_t", align_bytes=64)
+            for c in range(0, TOK, P):
+                d, s = weave_parts(g, c, c + P)
+                nc.gpsimd.tensor_scalar(out=d, in0=s, scalar1=1.0, scalar2=0.0, op0=ALU.mult, op1=ALU.add)
+
+        def quant_h(g):
+            if not 0 <= g < STEPS:
+                return
+            hq[g] = work.tile([P, TOK], U32, name="hq_t", align_bytes=64)
+            hs[g] = work.tile([P, TOK], U8, name="hs_t", align_bytes=64)
+            nc.vector.quantize_mx(out=hq[g][:].bitcast(FP8X4), scales=hs[g][:], in_=hg[g][:])
+
+        def mm2(g):
+            if not 0 <= g < STEPS:
+                return
+            o = o_pool.tile([P, J, N], F32, name="o_t")
+            ot[g] = o
+            for j in range(J):
+                nc.tensor.matmul_mx(out=o[:, j, :], lhsT=hq[g][:, j * P : (j + 1) * P].bitcast(FP8X4), lhsT_scale=hs[g][:, j * P : (j + 1) * P], rhs=w2_q[:].bitcast(FP8X4), rhs_scale=w2_s[:], start=True, stop=True)
+
+        def add_b2(g):
+            if not 0 <= g < STEPS:
+                return
+            m0[g] = tail.tile([P, J, N], F32, name="m0_t", align_bytes=64)
+            nc.vector.tensor_tensor(out=m0[g][:], in0=ot[g][:], in1=b2_f[:], op=ALU.add)
+
+        def mul_f(g):
+            if not 0 <= g < STEPS:
+                return
+            mm[g] = tail.tile([P, J * N], F32, name="mm_t", align_bytes=64)
+            nc.vector.tensor_tensor(out=mm[g][:], in0=m0[g][:].rearrange("p j n -> p (j n)"), in1=fb[g][:], op=ALU.mult)
+
+        def squares(g):
+            if not 0 <= g < STEPS:
+                return
+            if g % 2 == 0:
+                ss[g // 2] = tail.tile([P, 2 * J], F32, name="ss_t")
+            junk = work.tile([P, N], F32, name="junk_t", align_bytes=64)
+            for j in range(J):
+                c = (g % 2) * J + j
+                nc.scalar.activation(out=junk[:], in_=mm[g][:, j * N : (j + 1) * N], func=ACT.Square, accum_out=ss[g // 2][:, c : c + 1])
+
+        def clamp_a(q):
+            mx = tail.tile([P, 2 * J], F32, name="mx_t")
+            nc.vector.tensor_scalar(out=mx[:], in0=ss[q][:], scalar1=1.0, scalar2=None, op0=ALU.max)
+            return mx
+
+        def clamp_b(mx):
+            nr = tail.tile([P, 2 * J], F32, name="nr_t")
+            nc.scalar.activation(out=nr[:], in_=mx[:], func=ACT.Sqrt)
+            return nr
+
+        def clamp_c(q, nr):
+            fac[q] = tail.tile([P, 2 * J], F32, name="fac_t")
+            nc.vector.reciprocal(out=fac[q][:], in_=nr[:])
+
+        def finish(g):
+            if not 0 <= g < STEPS:
+                return
+            y = tail.tile([P, J * N], F32, name="y_t", align_bytes=64)
+            for j in range(J):
+                c = (g % 2) * J + j
+                nc.vector.tensor_scalar(out=y[:, j * N : (j + 1) * N], in0=mm[g][:, j * N : (j + 1) * N], scalar1=fac[g // 2][:, c : c + 1], scalar2=None, op0=ALU.mult)
+            nc.sync.dma_start(out=o_view[g], in_=y[:])
+
+        widen(0)
+        turn(0)
+        unturn(0)
+        nc.scalar.copy(out=nbias[:], in_=nb_raw[:])
+        nc.vector.tensor_copy(out=w1_g[:].rearrange("p (t m j) -> p t m j", t=4, j=4), in_=w1_raw[:].rearrange("p j (m t) -> p t m j", t=4))
+        widen(1)
+        turn(1)
+        nc.vector.tensor_copy(out=w2_g[:].rearrange("p (n j) -> p n j", j=4), in_=w2_raw[:].rearrange("p j n -> p n j"))
+        nc.vector.quantize_mx(out=w1_q[:].bitcast(FP8X4), scales=w1_s[:], in_=w1_g[:])
+        nc.vector.tensor_copy(out=b2_f[:, 0, :], in_=b2_raw[:])
+        nc.vector.quantize_mx(out=w2_q[:].bitcast(FP8X4), scales=w2_s[:], in_=w2_g[:])
+        for j in range(1, J):
+            nc.vector.tensor_copy(out=b2_f[:, j, :], in_=b2_f[:, 0, :])
+
+        for i in range(STEPS + 8):
+            fetch(i + 3)
+            quant_x(i)
+            mm1(i)
+            widen(i + 2)
+            mul_f(i - 3)
+            q = (i - 5) // 2
+            pair = i % 2 == 1 and 0 <= q < STEPS // 2
+            if pair:
+                nr = clamp_b(clamp_a(q))
+            relu(i)
+            finish(i - 6)
+            quant_h(i - 2)
+            mm2(i - 2)
+            weave(i - 1)
+            if pair:
+                clamp_c(q, nr)
+            unturn(i + 1)
+            add_b2(i - 2)
+            turn(i + 2)
+            squares(i - 3)

@@ -9,6 +9,8 @@ TOK = 512
 J = TOK // P
 STEPS = E // TOK
 FLOPS = 2 * E * H * (K + N)
+CAST_V = 0
+LAST = 30
 
 F32 = mybir.dt.float32
 BF16 = mybir.dt.bfloat16
@@ -28,11 +30,11 @@ def tile_filter_pa_t_kernel(tc, x_bytes, x_scale, f_weights, w1, node_bias, w2, 
 
     with ExitStack() as ctx:
         const = ctx.enter_context(tc.tile_pool(name="const", bufs=1))
-        load = ctx.enter_context(tc.tile_pool(name="load", bufs=5))
-        fload = ctx.enter_context(tc.tile_pool(name="fload", bufs=9))
+        load = ctx.enter_context(tc.tile_pool(name="load", bufs=4))
+        fload = ctx.enter_context(tc.tile_pool(name="fload", bufs=8))
         one = ctx.enter_context(tc.tile_pool(name="one", bufs=1))
         work = ctx.enter_context(tc.tile_pool(name="work", bufs=3))
-        tail = ctx.enter_context(tc.tile_pool(name="tail", bufs=6))
+        tail = ctx.enter_context(tc.tile_pool(name="tail", bufs=7))
         xt_pool = ctx.enter_context(tc.psum_pool(name="xt_pool", bufs=2))
         h_pool = ctx.enter_context(tc.psum_pool(name="h_pool", bufs=4))
         o_pool = ctx.enter_context(tc.psum_pool(name="o_pool", bufs=2))
@@ -41,28 +43,32 @@ def tile_filter_pa_t_kernel(tc, x_bytes, x_scale, f_weights, w1, node_bias, w2, 
         xb, fb = {}, {}
 
         def fetch(g):
-            if g >= STEPS:
+            if not 0 <= g < STEPS:
                 return
-            xb_t = load.tile([P, J * K], U8, name="xb_t", align_bytes=64)
-            nc.sync.dma_start(out=xb_t[:], in_=x_view[g])
-            xb[g] = xb_t
-            fb_t = fload.tile([P, J * N], BF16, name="fb_t", align_bytes=64)
-            nc.sync.dma_start(out=fb_t[:], in_=f_view[g])
-            fb[g] = fb_t
+            xb[g] = load.tile([P, J * K], U8, name="xb_t", align_bytes=64)
+            nc.sync.dma_start(out=xb[g][:], in_=x_view[g])
+
+        def fetch_f(g):
+            if not 0 <= g < STEPS:
+                return
+            fb[g] = fload.tile([P, J * N], BF16, name="fb_t", align_bytes=64)
+            nc.sync.dma_start(out=fb[g][:], in_=f_view[g])
 
         fetch(0)
         sc = const.tile([P, 4], F32, name="sc", align_bytes=64)
         nc.sync.dma_start(out=sc[:], in_=x_scale.rearrange("o (p t) -> p (o t)", t=4))
         w1_raw = const.tile([P, 4, H], BF16, name="w1_raw", align_bytes=64)
         nc.sync.dma_start(out=w1_raw[:], in_=w1.rearrange("(p j) c -> p j c", j=4))
+        fetch(1)
         nb_raw = const.tile([P, 4], BF16, name="nb_raw")
         nc.sync.dma_start(out=nb_raw[:], in_=node_bias.rearrange("(p t) -> p t", t=4))
-        fetch(1)
         w2_raw = const.tile([P, 4, N], BF16, name="w2_raw", align_bytes=64)
         nc.sync.dma_start(out=w2_raw[:], in_=w2.rearrange("(p j) n -> p j n", j=4))
         b2_raw = const.tile([P, N], BF16, name="b2_raw", align_bytes=64)
         nc.sync.dma_start(out=b2_raw[:], in_=b2.partition_broadcast(P))
+        fetch_f(0)
         fetch(2)
+        fetch_f(1)
 
         ident = const.tile([P, P], F32, name="ident", align_bytes=64)
         make_identity(nc, ident[:])
@@ -81,51 +87,54 @@ def tile_filter_pa_t_kernel(tc, x_bytes, x_scale, f_weights, w1, node_bias, w2, 
         w2_s = const.tile([P, N], U8, name="w2_s", align_bytes=64)
         b2_f = const.tile([P, J, N], F32, name="b2_f", align_bytes=64)
 
+        xw, xt, xg, xq, xs, ht, hp, hg, hq, hs, ot, ft, fs, m0, mm, ss, mx, nr, fac, yt = ({} for _ in range(20))
 
-        xw, xt, xg, xq, xs, ht, hp, hg, hq, hs, ot, m0, mm, ss, fac, yt = ({} for _ in range(16))
+        def ok(g):
+            return 0 <= g < STEPS
 
-        def widen(g):
-            if not 0 <= g < STEPS:
-                return
-            t = work.tile([P, J * K], BF16, name="xw_t", align_bytes=64)
-            xw[g] = t
-            nc.scalar.copy(out=t[:], in_=xb[g][:].bitcast(FP8))
+        def cast_v(g):
+            if ok(g):
+                xw[g] = work.tile([P, J * K], BF16, name="xw_t", align_bytes=64)
+                c = CAST_V if g else 1024
+                if c:
+                    nc.vector.tensor_copy(out=xw[g][:, :c], in_=xb[g][:, :c].bitcast(FP8))
 
-        def turn(g):
-            if not 0 <= g < STEPS:
+        def cast_s(g):
+            if ok(g):
+                c = CAST_V if g else 1024
+                nc.scalar.copy(out=xw[g][:, c:], in_=xb[g][:, c:].bitcast(FP8))
+
+        def turn(g, b):
+            if not ok(g):
                 return
             words = xw[g][:].bitcast(F32)
-            xt[g] = []
-            for b in range(2):
-                t = xt_pool.tile([P, 2, 2 * P], F32, name="xt_t")
-                for jj in range(2):
-                    j = 2 * b + jj
-                    for u in range(2):
-                        nc.tensor.transpose(t[:, u, jj * P : (jj + 1) * P], words[:, j * (K // 2) + u : (j + 1) * (K // 2) : 2], ident[:])
-                xt[g].append(t)
+            t = xt_pool.tile([P, 2, 2 * P], F32, name="xt_t")
+            for jj in range(2):
+                j = 2 * b + jj
+                for u in range(2):
+                    nc.tensor.transpose(t[:, u, jj * P : (jj + 1) * P], words[:, j * (K // 2) + u : (j + 1) * (K // 2) : 2], ident[:])
+            xt[g, b] = t
 
-        def unturn(g):
-            if not 0 <= g < STEPS:
+        def unturn(g, b):
+            if not ok(g):
                 return
-            t = work.tile([P, TOK * 4], BF16, name="xg_t", align_bytes=64)
-            xg[g] = t
-            for b in range(2):
-                nc.vector.tensor_tensor(
-                    out=t[:, b * 1024 : (b + 1) * 1024].rearrange("p (r u e) -> p r u e", u=2, e=2),
-                    in0=xt[g][b][:].rearrange("p u r -> p (u r)").bitcast(BF16).rearrange("p (u r e) -> p r u e", u=2, e=2),
-                    in1=sc[:].rearrange("p (o u e) -> p o u e", o=1, u=2).to_broadcast([P, 2 * P, 2, 2]),
-                    op=ALU.mult,
-                )
+            if b == 0:
+                xg[g] = work.tile([P, TOK * 4], BF16, name="xg_t", align_bytes=64)
+            nc.vector.tensor_tensor(
+                out=xg[g][:, b * 1024 : (b + 1) * 1024].rearrange("p (r u e) -> p r u e", u=2, e=2),
+                in0=xt[g, b][:].rearrange("p u r -> p (u r)").bitcast(BF16).rearrange("p (u r e) -> p r u e", u=2, e=2),
+                in1=sc[:].rearrange("p (o u e) -> p o u e", o=1, u=2).to_broadcast([P, 2 * P, 2, 2]),
+                op=ALU.mult,
+            )
 
         def quant_x(g):
-            if not 0 <= g < STEPS:
-                return
-            xq[g] = work.tile([P, TOK], U32, name="xq_t", align_bytes=64)
-            xs[g] = work.tile([P, TOK], U8, name="xs_t", align_bytes=64)
-            nc.vector.quantize_mx(out=xq[g][:].bitcast(FP8X4), scales=xs[g][:], in_=xg[g][:])
+            if ok(g):
+                xq[g] = work.tile([P, TOK], U32, name="xq_t", align_bytes=64)
+                xs[g] = work.tile([P, TOK], U8, name="xs_t", align_bytes=64)
+                nc.vector.quantize_mx(out=xq[g][:].bitcast(FP8X4), scales=xs[g][:], in_=xg[g][:])
 
         def mm1(g):
-            if not 0 <= g < STEPS:
+            if not ok(g):
                 return
             ht[g] = []
             for t in range(4):
@@ -133,118 +142,135 @@ def tile_filter_pa_t_kernel(tc, x_bytes, x_scale, f_weights, w1, node_bias, w2, 
                 nc.tensor.matmul_mx(out=h[:], lhsT=w1_q[:, t * P : (t + 1) * P].bitcast(FP8X4), lhsT_scale=w1_s[:, t * P : (t + 1) * P], rhs=xq[g][:].bitcast(FP8X4), rhs_scale=xs[g][:], start=True, stop=True)
                 ht[g].append(h)
 
-        def relu(g):
-            if not 0 <= g < STEPS:
+        def relu(g, ts):
+            if not ok(g):
                 return
-            hp[g] = work.tile([P, 4, TOK], BF16, name="hp_t", align_bytes=64)
-            for t in range(4):
-                nc.scalar.activation(out=hp[g][:, t, :], in_=ht[g][t][:], func=ACT.Relu, bias=nbias[:, t : t + 1])
-
-        def weave_parts(g, c0, c1):
-            dst = hg[g][:, 4 * c0 : 4 * c1].rearrange("p (c i t) -> p c t i", i=4, t=4)
-            src = hp[g][:, :, c0:c1].rearrange("p t (c i) -> p c t i", i=4)
-            return dst, src
+            if g not in hp:
+                hp[g] = work.tile([P, 4, TOK], BF16, name="hp_t", align_bytes=64)
+            for t in ts:
+                if t == 3 and g >= LAST + 2:
+                    nc.vector.tensor_scalar(out=hp[g][:, t, :], in0=ht[g][t][:], scalar1=nbias[:, t : t + 1], scalar2=0.0, op0=ALU.add, op1=ALU.max)
+                else:
+                    nc.scalar.activation(out=hp[g][:, t, :], in_=ht[g][t][:], func=ACT.Relu, bias=nbias[:, t : t + 1])
 
         def weave(g):
-            if not 0 <= g < STEPS:
+            if not ok(g):
                 return
             hg[g] = one.tile([P, TOK * 4], BF16, name="hg_t", align_bytes=64)
-            for c in range(0, TOK, P):
-                d, s = weave_parts(g, c, c + P)
-                nc.gpsimd.tensor_scalar(out=d, in0=s, scalar1=1.0, scalar2=0.0, op0=ALU.mult, op1=ALU.add)
+            for c in range(0, TOK, 128):
+                d = hg[g][:, 4 * c : 4 * c + 4 * 128].rearrange("p (c i t) -> p c t i", i=4, t=4)
+                s = hp[g][:, :, c : c + 128].rearrange("p t (c i) -> p c t i", i=4)
+                if g >= LAST:
+                    nc.vector.tensor_copy(out=d, in_=s)
+                else:
+                    nc.gpsimd.tensor_scalar(out=d, in0=s, scalar1=1.0, scalar2=0.0, op0=ALU.mult, op1=ALU.add)
 
         def quant_h(g):
-            if not 0 <= g < STEPS:
-                return
-            hq[g] = work.tile([P, TOK], U32, name="hq_t", align_bytes=64)
-            hs[g] = work.tile([P, TOK], U8, name="hs_t", align_bytes=64)
-            nc.vector.quantize_mx(out=hq[g][:].bitcast(FP8X4), scales=hs[g][:], in_=hg[g][:])
+            if ok(g):
+                hq[g] = work.tile([P, TOK], U32, name="hq_t", align_bytes=64)
+                hs[g] = work.tile([P, TOK], U8, name="hs_t", align_bytes=64)
+                nc.vector.quantize_mx(out=hq[g][:].bitcast(FP8X4), scales=hs[g][:], in_=hg[g][:])
 
         def mm2(g):
-            if not 0 <= g < STEPS:
-                return
-            o = o_pool.tile([P, J, N], F32, name="o_t")
-            ot[g] = o
-            for j in range(J):
-                nc.tensor.matmul_mx(out=o[:, j, :], lhsT=hq[g][:, j * P : (j + 1) * P].bitcast(FP8X4), lhsT_scale=hs[g][:, j * P : (j + 1) * P], rhs=w2_q[:].bitcast(FP8X4), rhs_scale=w2_s[:], start=True, stop=True)
+            if ok(g):
+                ot[g] = o_pool.tile([P, J, N], F32, name="o_t")
+                for j in range(J):
+                    nc.tensor.matmul_mx(out=ot[g][:, j, :], lhsT=hq[g][:, j * P : (j + 1) * P].bitcast(FP8X4), lhsT_scale=hs[g][:, j * P : (j + 1) * P], rhs=w2_q[:].bitcast(FP8X4), rhs_scale=w2_s[:], start=True, stop=True)
 
         def add_b2(g):
-            if not 0 <= g < STEPS:
-                return
-            m0[g] = tail.tile([P, J, N], F32, name="m0_t", align_bytes=64)
-            nc.vector.tensor_tensor(out=m0[g][:], in0=ot[g][:], in1=b2_f[:], op=ALU.add)
+            if ok(g):
+                m0[g] = work.tile([P, J * N], F32, name="m0_t", align_bytes=64)
+                nc.vector.tensor_tensor(out=m0[g][:], in0=ot[g][:].rearrange("p j n -> p (j n)"), in1=b2_f[:].rearrange("p j n -> p (j n)"), op=ALU.add)
 
         def mul_f(g):
-            if not 0 <= g < STEPS:
-                return
-            mm[g] = tail.tile([P, J * N], F32, name="mm_t", align_bytes=64)
-            nc.vector.tensor_tensor(out=mm[g][:], in0=m0[g][:].rearrange("p j n -> p (j n)"), in1=fb[g][:], op=ALU.mult)
+            if ok(g):
+                mm[g] = tail.tile([P, J * N], F32, name="mm_t", align_bytes=64)
+                nc.vector.tensor_tensor(out=mm[g][:], in0=m0[g][:], in1=fb[g][:], op=ALU.mult)
 
         def squares(g):
-            if not 0 <= g < STEPS:
-                return
-            if g % 2 == 0:
-                ss[g // 2] = tail.tile([P, 2 * J], F32, name="ss_t")
-            junk = work.tile([P, N], F32, name="junk_t", align_bytes=64)
-            for j in range(J):
-                c = (g % 2) * J + j
-                nc.scalar.activation(out=junk[:], in_=mm[g][:, j * N : (j + 1) * N], func=ACT.Square, accum_out=ss[g // 2][:, c : c + 1])
+            if ok(g):
+                if g % 2 == 0 or g >= LAST:
+                    ss[g] = tail.tile([P, 2 * J], F32, name="ss_t")
+                else:
+                    ss[g] = ss[g - 1]
+                junk = work.tile([P, N], F32, name="junk_t", align_bytes=64)
+                for j in range(J):
+                    c = col(g) + j
+                    nc.scalar.activation(out=junk[:], in_=mm[g][:, j * N : (j + 1) * N], func=ACT.Square, accum_out=ss[g][:, c : c + 1])
 
-        def clamp_a(q):
-            mx = tail.tile([P, 2 * J], F32, name="mx_t")
-            nc.vector.tensor_scalar(out=mx[:], in0=ss[q][:], scalar1=1.0, scalar2=None, op0=ALU.max)
-            return mx
+        def col(g):
+            return J * (g % 2) if g < LAST else 0
 
-        def clamp_b(mx):
-            nr = tail.tile([P, 2 * J], F32, name="nr_t")
-            nc.scalar.activation(out=nr[:], in_=mx[:], func=ACT.Sqrt)
-            return nr
+        def width(g):
+            return 2 * J if g < LAST else J
 
-        def clamp_c(q, nr):
-            fac[q] = tail.tile([P, 2 * J], F32, name="fac_t")
-            nc.vector.reciprocal(out=fac[q][:], in_=nr[:])
+        def clamp_a(g):
+            if ok(g) and (g % 2 == 1 or g >= LAST):
+                mx[g] = tail.tile([P, 2 * J], F32, name="mx_t")
+                nc.vector.tensor_scalar(out=mx[g][:, : width(g)], in0=ss[g][:, : width(g)], scalar1=1.0, scalar2=None, op0=ALU.max)
+
+        def clamp_b(g):
+            if ok(g) and (g % 2 == 1 or g >= LAST):
+                nr[g] = tail.tile([P, 2 * J], F32, name="nr_t")
+                nc.scalar.activation(out=nr[g][:, : width(g)], in_=mx[g][:, : width(g)], func=ACT.Sqrt)
+
+        def clamp_c(g):
+            if ok(g) and (g % 2 == 1 or g >= LAST):
+                fac[g] = tail.tile([P, 2 * J], F32, name="fac_t")
+                nc.vector.reciprocal(out=fac[g][:, : width(g)], in_=nr[g][:, : width(g)])
+                if g < LAST:
+                    fac[g - 1] = fac[g]
 
         def finish(g):
-            if not 0 <= g < STEPS:
+            if not ok(g):
                 return
             y = tail.tile([P, J * N], F32, name="y_t", align_bytes=64)
             for j in range(J):
-                c = (g % 2) * J + j
-                nc.vector.tensor_scalar(out=y[:, j * N : (j + 1) * N], in0=mm[g][:, j * N : (j + 1) * N], scalar1=fac[g // 2][:, c : c + 1], scalar2=None, op0=ALU.mult)
+                f = fac[g][:, col(g) + j : col(g) + j + 1]
+                if False:
+                    nc.vector.tensor_scalar(out=y[:, j * N : (j + 1) * N], in0=mm[g][:, j * N : (j + 1) * N], scalar1=f, scalar2=None, op0=ALU.mult)
+                else:
+                    nc.scalar.activation(out=y[:, j * N : (j + 1) * N], in_=mm[g][:, j * N : (j + 1) * N], func=ACT.Copy, scale=f)
             nc.sync.dma_start(out=o_view[g], in_=y[:])
 
-        widen(0)
-        turn(0)
-        unturn(0)
+        cast_v(0)
+        cast_s(0)
+        for b in range(2):
+            turn(0, b)
+        cast_v(1)
+        cast_s(1)
         nc.scalar.copy(out=nbias[:], in_=nb_raw[:])
         nc.vector.tensor_copy(out=w1_g[:].rearrange("p (t m j) -> p t m j", t=4, j=4), in_=w1_raw[:].rearrange("p j (m t) -> p t m j", t=4))
-        widen(1)
-        turn(1)
-        nc.vector.tensor_copy(out=w2_g[:].rearrange("p (n j) -> p n j", j=4), in_=w2_raw[:].rearrange("p j n -> p n j"))
+        for b in range(2):
+            unturn(0, b)
+            turn(1, b)
         nc.vector.quantize_mx(out=w1_q[:].bitcast(FP8X4), scales=w1_s[:], in_=w1_g[:])
-        nc.vector.tensor_copy(out=b2_f[:, 0, :], in_=b2_raw[:])
-        nc.vector.quantize_mx(out=w2_q[:].bitcast(FP8X4), scales=w2_s[:], in_=w2_g[:])
-        for j in range(1, J):
-            nc.vector.tensor_copy(out=b2_f[:, j, :], in_=b2_f[:, 0, :])
 
         for i in range(STEPS + 8):
             fetch(i + 3)
+            fetch_f(i + 2)
             quant_x(i)
             mm1(i)
-            widen(i + 2)
+            cast_v(i + 2)
+            if i == 0:
+                nc.vector.tensor_copy(out=w2_g[:].rearrange("p (n j) -> p n j", j=4), in_=w2_raw[:].rearrange("p j n -> p n j"))
+                for j in range(J):
+                    nc.vector.tensor_copy(out=b2_f[:, j, :], in_=b2_raw[:])
+                nc.vector.quantize_mx(out=w2_q[:].bitcast(FP8X4), scales=w2_s[:], in_=w2_g[:])
+            cast_s(i + 2)
             mul_f(i - 3)
-            q = (i - 5) // 2
-            pair = i % 2 == 1 and 0 <= q < STEPS // 2
-            if pair:
-                nr = clamp_b(clamp_a(q))
-            relu(i)
-            finish(i - 6)
+            clamp_a(i - 4)
             quant_h(i - 2)
             mm2(i - 2)
-            weave(i - 1)
-            if pair:
-                clamp_c(q, nr)
-            unturn(i + 1)
-            add_b2(i - 2)
-            turn(i + 2)
+            clamp_b(i - 4)
+            relu(i, (0, 1))
             squares(i - 3)
+            weave(i - 1)
+            unturn(i + 1, 0)
+            turn(i + 2, 0)
+            clamp_c(i - 4)
+            relu(i, (2, 3))
+            finish(i - 6)
+            unturn(i + 1, 1)
+            turn(i + 2, 1)
+            add_b2(i - 2)

@@ -9,7 +9,6 @@ TOK = 512
 J = TOK // P
 STEPS = E // TOK
 FLOPS = 2 * E * H * (K + N)
-CAST_V = 0
 LAST = 30
 
 F32 = mybir.dt.float32
@@ -30,14 +29,16 @@ def tile_filter_pa_t_kernel(tc, x_bytes, x_scale, f_weights, w1, node_bias, w2, 
 
     with ExitStack() as ctx:
         const = ctx.enter_context(tc.tile_pool(name="const", bufs=1))
-        load = ctx.enter_context(tc.tile_pool(name="load", bufs=4))
-        fload = ctx.enter_context(tc.tile_pool(name="fload", bufs=8))
+        load = ctx.enter_context(tc.tile_pool(name="load", bufs=6))
+        fload = ctx.enter_context(tc.tile_pool(name="fload", bufs=7))
         one = ctx.enter_context(tc.tile_pool(name="one", bufs=1))
         work = ctx.enter_context(tc.tile_pool(name="work", bufs=3))
-        tail = ctx.enter_context(tc.tile_pool(name="tail", bufs=7))
+        tail = ctx.enter_context(tc.tile_pool(name="tail", bufs=4))
         xt_pool = ctx.enter_context(tc.psum_pool(name="xt_pool", bufs=2))
-        h_pool = ctx.enter_context(tc.psum_pool(name="h_pool", bufs=4))
-        o_pool = ctx.enter_context(tc.psum_pool(name="o_pool", bufs=2))
+        h_pool = ctx.enter_context(tc.psum_pool(name="h_pool", bufs=3))
+        o_pool = ctx.enter_context(tc.psum_pool(name="o_pool", bufs=1))
+        f_pool = ctx.enter_context(tc.psum_pool(name="f_pool", bufs=1))
+        m_pool = ctx.enter_context(tc.psum_pool(name="m_pool", bufs=1))
         ctx.enter_context(tc.manual_schedule())
 
         xb, fb = {}, {}
@@ -64,19 +65,25 @@ def tile_filter_pa_t_kernel(tc, x_bytes, x_scale, f_weights, w1, node_bias, w2, 
         nc.sync.dma_start(out=nb_raw[:], in_=node_bias.rearrange("(p t) -> p t", t=4))
         w2_raw = const.tile([P, 4, N], BF16, name="w2_raw", align_bytes=64)
         nc.sync.dma_start(out=w2_raw[:], in_=w2.rearrange("(p j) n -> p j n", j=4))
-        b2_raw = const.tile([P, N], BF16, name="b2_raw", align_bytes=64)
-        nc.sync.dma_start(out=b2_raw[:], in_=b2.partition_broadcast(P))
+        b2_raw = const.tile([P, 2], BF16, name="b2_raw", align_bytes=64)
+        nc.sync.dma_start(out=b2_raw[:, 0:1], in_=b2.rearrange("(p o) -> p o", o=1))
         fetch_f(0)
         fetch(2)
         fetch_f(1)
+        fetch(3)
+        fetch_f(2)
 
         ident = const.tile([P, P], F32, name="ident", align_bytes=64)
         make_identity(nc, ident[:])
+        ident_b = const.tile([P, P], BF16, name="ident_b", align_bytes=64)
+        nc.gpsimd.tensor_copy(out=ident_b[:], in_=ident[:])
 
         warm = const.tile([P, 1], F32, name="warm")
         nc.vector.memset(warm[:], 1.0)
+        minus_one = const.tile([P, 1], F32, name="minus_one")
+        nc.vector.memset(minus_one[:], -1.0)
         warm2 = const.tile([P, 1], F32, name="warm2")
-        nc.scalar.activation(out=warm2[:], in_=warm[:], func=ACT.Sqrt)
+        nc.scalar.activation(out=warm2[:], in_=warm[:], func=ACT.Abs_reciprocal_sqrt)
 
         nbias = const.tile([P, 4], F32, name="nbias")
         w1_g = const.tile([P, 4 * H], BF16, name="w1_g", align_bytes=64)
@@ -85,24 +92,37 @@ def tile_filter_pa_t_kernel(tc, x_bytes, x_scale, f_weights, w1, node_bias, w2, 
         w2_g = const.tile([P, 4 * N], BF16, name="w2_g", align_bytes=64)
         w2_q = const.tile([P, N], U32, name="w2_q", align_bytes=64)
         w2_s = const.tile([P, N], U8, name="w2_s", align_bytes=64)
-        b2_f = const.tile([P, J, N], F32, name="b2_f", align_bytes=64)
+        b2_f = const.tile([P, 1], F32, name="b2_f")
 
-        xw, xt, xg, xq, xs, ht, hp, hg, hq, hs, ot, ft, fs, m0, mm, ss, mx, nr, fac, yt = ({} for _ in range(20))
+        xw, xt, xg, xq, xs, ht, hp, hg, hq, hs, ot, ft, fs, mt, mp, ss, mx, nr, fac, yt = ({} for _ in range(20))
 
         def ok(g):
             return 0 <= g < STEPS
 
+        def vector_cols(g):
+            if g == 0:
+                return 0
+            if g == 1:
+                return 0
+            return 512 if g >= STEPS - 0 else 1280
+
+        def wide(g):
+            if g not in xw:
+                xw[g] = work.tile([P, J * K], BF16, name="xw_t", align_bytes=64)
+
         def cast_v(g):
             if ok(g):
-                xw[g] = work.tile([P, J * K], BF16, name="xw_t", align_bytes=64)
-                c = CAST_V if g else 1024
+                wide(g)
+                c = vector_cols(g)
                 if c:
                     nc.vector.tensor_copy(out=xw[g][:, :c], in_=xb[g][:, :c].bitcast(FP8))
 
         def cast_s(g):
             if ok(g):
-                c = CAST_V if g else 1024
-                nc.scalar.copy(out=xw[g][:, c:], in_=xb[g][:, c:].bitcast(FP8))
+                wide(g)
+                c = vector_cols(g)
+                if c < J * K:
+                    nc.scalar.copy(out=xw[g][:, c:], in_=xb[g][:, c:].bitcast(FP8))
 
         def turn(g, b):
             if not ok(g):
@@ -118,7 +138,7 @@ def tile_filter_pa_t_kernel(tc, x_bytes, x_scale, f_weights, w1, node_bias, w2, 
         def unturn(g, b):
             if not ok(g):
                 return
-            if b == 0:
+            if g not in xg:
                 xg[g] = work.tile([P, TOK * 4], BF16, name="xg_t", align_bytes=64)
             nc.vector.tensor_tensor(
                 out=xg[g][:, b * 1024 : (b + 1) * 1024].rearrange("p (r u e) -> p r u e", u=2, e=2),
@@ -133,14 +153,12 @@ def tile_filter_pa_t_kernel(tc, x_bytes, x_scale, f_weights, w1, node_bias, w2, 
                 xs[g] = work.tile([P, TOK], U8, name="xs_t", align_bytes=64)
                 nc.vector.quantize_mx(out=xq[g][:].bitcast(FP8X4), scales=xs[g][:], in_=xg[g][:])
 
-        def mm1(g):
+        def mm1(g, ts):
             if not ok(g):
                 return
-            ht[g] = []
-            for t in range(4):
-                h = h_pool.tile([P, TOK], F32, name="h_t")
-                nc.tensor.matmul_mx(out=h[:], lhsT=w1_q[:, t * P : (t + 1) * P].bitcast(FP8X4), lhsT_scale=w1_s[:, t * P : (t + 1) * P], rhs=xq[g][:].bitcast(FP8X4), rhs_scale=xs[g][:], start=True, stop=True)
-                ht[g].append(h)
+            for t in ts:
+                ht[g, t] = h_pool.tile([P, TOK], F32, name="h_t")
+                nc.tensor.matmul_mx(out=ht[g, t][:], lhsT=w1_q[:, t * P : (t + 1) * P].bitcast(FP8X4), lhsT_scale=w1_s[:, t * P : (t + 1) * P], rhs=xq[g][:].bitcast(FP8X4), rhs_scale=xs[g][:], start=True, stop=True)
 
         def relu(g, ts):
             if not ok(g):
@@ -148,22 +166,30 @@ def tile_filter_pa_t_kernel(tc, x_bytes, x_scale, f_weights, w1, node_bias, w2, 
             if g not in hp:
                 hp[g] = work.tile([P, 4, TOK], BF16, name="hp_t", align_bytes=64)
             for t in ts:
-                if t == 3 and g >= LAST + 2:
-                    nc.vector.tensor_scalar(out=hp[g][:, t, :], in0=ht[g][t][:], scalar1=nbias[:, t : t + 1], scalar2=0.0, op0=ALU.add, op1=ALU.max)
+                if g == STEPS - 1 and "SSSV"[t] == "V":
+                    nc.vector.tensor_scalar(out=hp[g][:, t, :], in0=ht[g, t][:], scalar1=nbias[:, t : t + 1], scalar2=0.0, op0=ALU.add, op1=ALU.max)
                 else:
-                    nc.scalar.activation(out=hp[g][:, t, :], in_=ht[g][t][:], func=ACT.Relu, bias=nbias[:, t : t + 1])
+                    nc.scalar.activation(out=hp[g][:, t, :], in_=ht[g, t][:], func=ACT.Relu, bias=nbias[:, t : t + 1])
+
+        def weave_part(engine, g, c0, c1):
+            d = hg[g][:, 4 * c0 : 4 * c1].rearrange("p (c i t) -> p c t i", i=4, t=4)
+            s = hp[g][:, :, c0:c1].rearrange("p t (c i) -> p c t i", i=4)
+            if engine == "gpsimd":
+                nc.gpsimd.tensor_scalar(out=d, in0=s, scalar1=1.0, scalar2=0.0, op0=ALU.mult, op1=ALU.add)
+            elif engine == "vector":
+                nc.vector.tensor_copy(out=d, in_=s)
+            else:
+                nc.scalar.copy(out=d, in_=s)
 
         def weave(g):
             if not ok(g):
                 return
             hg[g] = one.tile([P, TOK * 4], BF16, name="hg_t", align_bytes=64)
-            for c in range(0, TOK, 128):
-                d = hg[g][:, 4 * c : 4 * c + 4 * 128].rearrange("p (c i t) -> p c t i", i=4, t=4)
-                s = hp[g][:, :, c : c + 128].rearrange("p t (c i) -> p c t i", i=4)
-                if g >= LAST:
-                    nc.vector.tensor_copy(out=d, in_=s)
-                else:
-                    nc.gpsimd.tensor_scalar(out=d, in0=s, scalar1=1.0, scalar2=0.0, op0=ALU.mult, op1=ALU.add)
+            if g >= LAST:
+                weave_part("vector", g, 0, 512)
+            else:
+                for c in range(0, TOK, 512):
+                    weave_part("gpsimd", g, c, c + 512)
 
         def quant_h(g):
             if ok(g):
@@ -173,104 +199,96 @@ def tile_filter_pa_t_kernel(tc, x_bytes, x_scale, f_weights, w1, node_bias, w2, 
 
         def mm2(g):
             if ok(g):
-                ot[g] = o_pool.tile([P, J, N], F32, name="o_t")
+                ot[g] = o_pool.tile([P, TOK], F32, name="o_t")
+                nc.tensor.matmul_mx(out=ot[g][:], lhsT=w2_q[:].bitcast(FP8X4), lhsT_scale=w2_s[:], rhs=hq[g][:].bitcast(FP8X4), rhs_scale=hs[g][:], start=True, stop=True)
+
+        def turn_f(g):
+            if ok(g):
+                ft[g] = f_pool.tile([P, TOK], BF16, name="ft_t")
                 for j in range(J):
-                    nc.tensor.matmul_mx(out=ot[g][:, j, :], lhsT=hq[g][:, j * P : (j + 1) * P].bitcast(FP8X4), lhsT_scale=hs[g][:, j * P : (j + 1) * P], rhs=w2_q[:].bitcast(FP8X4), rhs_scale=w2_s[:], start=True, stop=True)
+                    nc.tensor.transpose(ft[g][:, j * P : (j + 1) * P], fb[g][:, j * N : (j + 1) * N], ident_b[:])
 
-        def add_b2(g):
+        def copy_f(g):
             if ok(g):
-                m0[g] = work.tile([P, J * N], F32, name="m0_t", align_bytes=64)
-                nc.vector.tensor_tensor(out=m0[g][:], in0=ot[g][:].rearrange("p j n -> p (j n)"), in1=b2_f[:].rearrange("p j n -> p (j n)"), op=ALU.add)
+                fs[g] = work.tile([P, TOK], BF16, name="fs_t", align_bytes=64)
+                nc.scalar.copy(out=fs[g][:], in_=ft[g][:])
 
-        def mul_f(g):
+        def message(g):
             if ok(g):
-                mm[g] = tail.tile([P, J * N], F32, name="mm_t", align_bytes=64)
-                nc.vector.tensor_tensor(out=mm[g][:], in0=m0[g][:], in1=fb[g][:], op=ALU.mult)
+                mt[g] = tail.tile([P, TOK], F32, name="mt_t", align_bytes=64)
+                nc.vector.scalar_tensor_tensor(out=mt[g][:], in0=ot[g][:], scalar=b2_f[:], in1=fs[g][:], op0=ALU.add, op1=ALU.mult)
+
+        def turn_m(g):
+            if ok(g):
+                mp[g] = m_pool.tile([P, J, N], F32, name="mp_t")
+                for j in range(J):
+                    nc.tensor.transpose(mp[g][:, j, :], mt[g][:, j * P : (j + 1) * P], ident[:])
 
         def squares(g):
             if ok(g):
-                if g % 2 == 0 or g >= LAST:
-                    ss[g] = tail.tile([P, 2 * J], F32, name="ss_t")
-                else:
-                    ss[g] = ss[g - 1]
+                ss[g] = tail.tile([P, J], F32, name="ss_t")
                 junk = work.tile([P, N], F32, name="junk_t", align_bytes=64)
                 for j in range(J):
-                    c = col(g) + j
-                    nc.scalar.activation(out=junk[:], in_=mm[g][:, j * N : (j + 1) * N], func=ACT.Square, accum_out=ss[g][:, c : c + 1])
-
-        def col(g):
-            return J * (g % 2) if g < LAST else 0
-
-        def width(g):
-            return 2 * J if g < LAST else J
+                    nc.scalar.activation(out=junk[:], in_=mp[g][:, j, :], func=ACT.Square, accum_out=ss[g][:, j : j + 1])
 
         def clamp_a(g):
-            if ok(g) and (g % 2 == 1 or g >= LAST):
-                mx[g] = tail.tile([P, 2 * J], F32, name="mx_t")
-                nc.vector.tensor_scalar(out=mx[g][:, : width(g)], in0=ss[g][:, : width(g)], scalar1=1.0, scalar2=None, op0=ALU.max)
+            if ok(g):
+                nr[g] = tail.tile([P, J], F32, name="nr_t")
+                nc.scalar.activation(out=nr[g][:], in_=ss[g][:], func=ACT.Relu, bias=minus_one[:])
 
         def clamp_b(g):
-            if ok(g) and (g % 2 == 1 or g >= LAST):
-                nr[g] = tail.tile([P, 2 * J], F32, name="nr_t")
-                nc.scalar.activation(out=nr[g][:, : width(g)], in_=mx[g][:, : width(g)], func=ACT.Sqrt)
-
-        def clamp_c(g):
-            if ok(g) and (g % 2 == 1 or g >= LAST):
-                fac[g] = tail.tile([P, 2 * J], F32, name="fac_t")
-                nc.vector.reciprocal(out=fac[g][:, : width(g)], in_=nr[g][:, : width(g)])
-                if g < LAST:
-                    fac[g - 1] = fac[g]
+            if ok(g):
+                fac[g] = tail.tile([P, J], F32, name="fac_t")
+                nc.scalar.activation(out=fac[g][:], in_=nr[g][:], func=ACT.Abs_reciprocal_sqrt, bias=warm[:])
 
         def finish(g):
             if not ok(g):
                 return
             y = tail.tile([P, J * N], F32, name="y_t", align_bytes=64)
             for j in range(J):
-                f = fac[g][:, col(g) + j : col(g) + j + 1]
-                if False:
-                    nc.vector.tensor_scalar(out=y[:, j * N : (j + 1) * N], in0=mm[g][:, j * N : (j + 1) * N], scalar1=f, scalar2=None, op0=ALU.mult)
-                else:
-                    nc.scalar.activation(out=y[:, j * N : (j + 1) * N], in_=mm[g][:, j * N : (j + 1) * N], func=ACT.Copy, scale=f)
+                nc.scalar.activation(out=y[:, j * N : (j + 1) * N], in_=mp[g][:, j, :], func=ACT.Copy, scale=fac[g][:, j : j + 1])
             nc.sync.dma_start(out=o_view[g], in_=y[:])
 
-        cast_v(0)
-        cast_s(0)
-        for b in range(2):
-            turn(0, b)
-        cast_v(1)
-        cast_s(1)
         nc.scalar.copy(out=nbias[:], in_=nb_raw[:])
+        cast_s(0)
+        turn(0, 1)
+        cast_s(1)
+        turn(0, 0)
         nc.vector.tensor_copy(out=w1_g[:].rearrange("p (t m j) -> p t m j", t=4, j=4), in_=w1_raw[:].rearrange("p j (m t) -> p t m j", t=4))
-        for b in range(2):
-            unturn(0, b)
-            turn(1, b)
         nc.vector.quantize_mx(out=w1_q[:].bitcast(FP8X4), scales=w1_s[:], in_=w1_g[:])
+        cast_v(1)
+        unturn(0, 1)
+        turn(1, 0)
+        unturn(0, 0)
+        turn(1, 1)
+        cast_v(0)
 
-        for i in range(STEPS + 8):
-            fetch(i + 3)
-            fetch_f(i + 2)
-            quant_x(i)
-            mm1(i)
+        for i in range(STEPS + 3):
+            fetch(i + 4)
+            fetch_f(i + 3)
+            squares(i - 3)
             cast_v(i + 2)
             if i == 0:
                 nc.vector.tensor_copy(out=w2_g[:].rearrange("p (n j) -> p n j", j=4), in_=w2_raw[:].rearrange("p j n -> p n j"))
-                for j in range(J):
-                    nc.vector.tensor_copy(out=b2_f[:, j, :], in_=b2_raw[:])
+                nc.vector.tensor_copy(out=b2_f[:], in_=b2_raw[:, 0:1])
                 nc.vector.quantize_mx(out=w2_q[:].bitcast(FP8X4), scales=w2_s[:], in_=w2_g[:])
             cast_s(i + 2)
-            mul_f(i - 3)
-            clamp_a(i - 4)
+            turn_f(i)
             quant_h(i - 2)
-            mm2(i - 2)
-            clamp_b(i - 4)
-            relu(i, (0, 1))
-            squares(i - 3)
+            clamp_a(i - 3)
+            quant_x(i)
             weave(i - 1)
+            mm1(i, (0, 1))
+            mm2(i - 2)
+            copy_f(i)
             unturn(i + 1, 0)
-            turn(i + 2, 0)
-            clamp_c(i - 4)
-            relu(i, (2, 3))
-            finish(i - 6)
+            clamp_b(i - 3)
             unturn(i + 1, 1)
+            relu(i, (0, 1))
+            mm1(i, (2, 3))
+            message(i - 2)
+            finish(i - 3)
+            relu(i, (2, 3))
+            turn(i + 2, 0)
+            turn_m(i - 2)
             turn(i + 2, 1)
-            add_b2(i - 2)

@@ -9,7 +9,7 @@ TOK = 512
 J = TOK // P
 STEPS = E // TOK
 FLOPS = 2 * E * H * (K + N)
-LAST = 30
+LAST = 32
 
 F32 = mybir.dt.float32
 BF16 = mybir.dt.bfloat16
@@ -30,15 +30,14 @@ def tile_filter_pa_t_kernel(tc, x_bytes, x_scale, f_weights, w1, node_bias, w2, 
     with ExitStack() as ctx:
         const = ctx.enter_context(tc.tile_pool(name="const", bufs=1))
         load = ctx.enter_context(tc.tile_pool(name="load", bufs=6))
-        fload = ctx.enter_context(tc.tile_pool(name="fload", bufs=7))
+        fload = ctx.enter_context(tc.tile_pool(name="fload", bufs=9))
         one = ctx.enter_context(tc.tile_pool(name="one", bufs=1))
         work = ctx.enter_context(tc.tile_pool(name="work", bufs=3))
-        tail = ctx.enter_context(tc.tile_pool(name="tail", bufs=4))
+        tail = ctx.enter_context(tc.tile_pool(name="tail", bufs=8))
         xt_pool = ctx.enter_context(tc.psum_pool(name="xt_pool", bufs=2))
         h_pool = ctx.enter_context(tc.psum_pool(name="h_pool", bufs=3))
         o_pool = ctx.enter_context(tc.psum_pool(name="o_pool", bufs=1))
-        f_pool = ctx.enter_context(tc.psum_pool(name="f_pool", bufs=1))
-        m_pool = ctx.enter_context(tc.psum_pool(name="m_pool", bufs=1))
+        m_pool = ctx.enter_context(tc.psum_pool(name="m_pool", bufs=2))
         ctx.enter_context(tc.manual_schedule())
 
         xb, fb = {}, {}
@@ -75,8 +74,6 @@ def tile_filter_pa_t_kernel(tc, x_bytes, x_scale, f_weights, w1, node_bias, w2, 
 
         ident = const.tile([P, P], F32, name="ident", align_bytes=64)
         make_identity(nc, ident[:])
-        ident_b = const.tile([P, P], BF16, name="ident_b", align_bytes=64)
-        nc.gpsimd.tensor_copy(out=ident_b[:], in_=ident[:])
 
         warm = const.tile([P, 1], F32, name="warm")
         nc.vector.memset(warm[:], 1.0)
@@ -94,17 +91,17 @@ def tile_filter_pa_t_kernel(tc, x_bytes, x_scale, f_weights, w1, node_bias, w2, 
         w2_s = const.tile([P, N], U8, name="w2_s", align_bytes=64)
         b2_f = const.tile([P, 1], F32, name="b2_f")
 
-        xw, xt, xg, xq, xs, ht, hp, hg, hq, hs, ot, ft, fs, mt, mp, ss, mx, nr, fac, yt = ({} for _ in range(20))
+        xw, xt, xg, xq, xs, ht, hp, hg, hq, hs, ot, m0, mp, mm, ss, nr, fac = ({} for _ in range(17))
 
         def ok(g):
             return 0 <= g < STEPS
 
         def vector_cols(g):
             if g == 0:
-                return 0
+                return 1536
             if g == 1:
                 return 0
-            return 512 if g >= STEPS - 0 else 1280
+            return 0 if g >= STEPS - 1 else 768
 
         def wide(g):
             if g not in xw:
@@ -166,7 +163,7 @@ def tile_filter_pa_t_kernel(tc, x_bytes, x_scale, f_weights, w1, node_bias, w2, 
             if g not in hp:
                 hp[g] = work.tile([P, 4, TOK], BF16, name="hp_t", align_bytes=64)
             for t in ts:
-                if g == STEPS - 1 and "SSSV"[t] == "V":
+                if g == STEPS - 1 and "SSSS"[t] == "V":
                     nc.vector.tensor_scalar(out=hp[g][:, t, :], in0=ht[g, t][:], scalar1=nbias[:, t : t + 1], scalar2=0.0, op0=ALU.add, op1=ALU.max)
                 else:
                     nc.scalar.activation(out=hp[g][:, t, :], in_=ht[g, t][:], func=ACT.Relu, bias=nbias[:, t : t + 1])
@@ -202,93 +199,108 @@ def tile_filter_pa_t_kernel(tc, x_bytes, x_scale, f_weights, w1, node_bias, w2, 
                 ot[g] = o_pool.tile([P, TOK], F32, name="o_t")
                 nc.tensor.matmul_mx(out=ot[g][:], lhsT=w2_q[:].bitcast(FP8X4), lhsT_scale=w2_s[:], rhs=hq[g][:].bitcast(FP8X4), rhs_scale=hs[g][:], start=True, stop=True)
 
-        def turn_f(g):
+        def add_b2(g):
             if ok(g):
-                ft[g] = f_pool.tile([P, TOK], BF16, name="ft_t")
+                m0[g] = work.tile([P, TOK], F32, name="m0_t", align_bytes=64)
+                nc.vector.tensor_scalar(out=m0[g][:], in0=ot[g][:], scalar1=b2_f[:], scalar2=None, op0=ALU.add)
+
+        def turn_o(g):
+            if ok(g):
+                mp[g] = m_pool.tile([P, J * N], F32, name="mp_t")
                 for j in range(J):
-                    nc.tensor.transpose(ft[g][:, j * P : (j + 1) * P], fb[g][:, j * N : (j + 1) * N], ident_b[:])
+                    nc.tensor.transpose(mp[g][:, j * N : (j + 1) * N], m0[g][:, j * P : (j + 1) * P], ident[:])
 
-        def copy_f(g):
+        def mul_f(g):
             if ok(g):
-                fs[g] = work.tile([P, TOK], BF16, name="fs_t", align_bytes=64)
-                nc.scalar.copy(out=fs[g][:], in_=ft[g][:])
+                mm[g] = tail.tile([P, J * N], F32, name="mm_t", align_bytes=64)
+                nc.vector.tensor_tensor(out=mm[g][:], in0=mp[g][:], in1=fb[g][:], op=ALU.mult)
 
-        def message(g):
-            if ok(g):
-                mt[g] = tail.tile([P, TOK], F32, name="mt_t", align_bytes=64)
-                nc.vector.scalar_tensor_tensor(out=mt[g][:], in0=ot[g][:], scalar=b2_f[:], in1=fs[g][:], op0=ALU.add, op1=ALU.mult)
+        def paired(g):
+            return g < STEPS - 2
 
-        def turn_m(g):
-            if ok(g):
-                mp[g] = m_pool.tile([P, J, N], F32, name="mp_t")
-                for j in range(J):
-                    nc.tensor.transpose(mp[g][:, j, :], mt[g][:, j * P : (j + 1) * P], ident[:])
+        def last_of_group(g):
+            return g % 2 == 1 or not paired(g)
+
+        def col(g):
+            return J * (g % 2) if paired(g) else 0
+
+        def width(g):
+            return 2 * J if paired(g) else J
 
         def squares(g):
-            if ok(g):
-                ss[g] = tail.tile([P, J], F32, name="ss_t")
-                junk = work.tile([P, N], F32, name="junk_t", align_bytes=64)
-                for j in range(J):
-                    nc.scalar.activation(out=junk[:], in_=mp[g][:, j, :], func=ACT.Square, accum_out=ss[g][:, j : j + 1])
+            if not ok(g):
+                return
+            if paired(g) and g % 2 == 1:
+                ss[g] = ss[g - 1]
+            else:
+                ss[g] = tail.tile([P, 2 * J], F32, name="ss_t")
+            junk = work.tile([P, N], F32, name="junk_t", align_bytes=64)
+            for j in range(J):
+                c = col(g) + j
+                nc.scalar.activation(out=junk[:], in_=mm[g][:, j * N : (j + 1) * N], func=ACT.Square, accum_out=ss[g][:, c : c + 1])
 
         def clamp_a(g):
-            if ok(g):
-                nr[g] = tail.tile([P, J], F32, name="nr_t")
-                nc.scalar.activation(out=nr[g][:], in_=ss[g][:], func=ACT.Relu, bias=minus_one[:])
+            if ok(g) and last_of_group(g):
+                nr[g] = tail.tile([P, 2 * J], F32, name="nr_t")
+                nc.scalar.activation(out=nr[g][:, : width(g)], in_=ss[g][:, : width(g)], func=ACT.Relu, bias=minus_one[:])
 
         def clamp_b(g):
-            if ok(g):
-                fac[g] = tail.tile([P, J], F32, name="fac_t")
-                nc.scalar.activation(out=fac[g][:], in_=nr[g][:], func=ACT.Abs_reciprocal_sqrt, bias=warm[:])
+            if ok(g) and last_of_group(g):
+                fac[g] = tail.tile([P, 2 * J], F32, name="fac_t")
+                nc.scalar.activation(out=fac[g][:, : width(g)], in_=nr[g][:, : width(g)], func=ACT.Abs_reciprocal_sqrt, bias=warm[:])
+                if paired(g):
+                    fac[g - 1] = fac[g]
 
         def finish(g):
             if not ok(g):
                 return
             y = tail.tile([P, J * N], F32, name="y_t", align_bytes=64)
             for j in range(J):
-                nc.scalar.activation(out=y[:, j * N : (j + 1) * N], in_=mp[g][:, j, :], func=ACT.Copy, scale=fac[g][:, j : j + 1])
+                f = fac[g][:, col(g) + j : col(g) + j + 1]
+                nc.scalar.activation(out=y[:, j * N : (j + 1) * N], in_=mm[g][:, j * N : (j + 1) * N], func=ACT.Copy, scale=f)
             nc.sync.dma_start(out=o_view[g], in_=y[:])
 
         nc.scalar.copy(out=nbias[:], in_=nb_raw[:])
         cast_s(0)
-        turn(0, 1)
         cast_s(1)
-        turn(0, 0)
-        nc.vector.tensor_copy(out=w1_g[:].rearrange("p (t m j) -> p t m j", t=4, j=4), in_=w1_raw[:].rearrange("p j (m t) -> p t m j", t=4))
-        nc.vector.quantize_mx(out=w1_q[:].bitcast(FP8X4), scales=w1_s[:], in_=w1_g[:])
         cast_v(1)
+        cast_v(0)
+        nc.vector.tensor_copy(out=w1_g[:].rearrange("p (t m j) -> p t m j", t=4, j=4), in_=w1_raw[:].rearrange("p j (m t) -> p t m j", t=4))
+        turn(0, 1)
         unturn(0, 1)
+        turn(0, 0)
         turn(1, 0)
+        nc.vector.quantize_mx(out=w1_q[:].bitcast(FP8X4), scales=w1_s[:], in_=w1_g[:])
         unturn(0, 0)
         turn(1, 1)
-        cast_v(0)
 
-        for i in range(STEPS + 3):
+        for i in range(STEPS + 6):
             fetch(i + 4)
             fetch_f(i + 3)
-            squares(i - 3)
+            if i > 0:
+                unturn(i, 1)
+            relu(i - 1, (2, 3))
+            if i + 1 > 1:
+                turn(i + 1, 1)
             cast_v(i + 2)
             if i == 0:
                 nc.vector.tensor_copy(out=w2_g[:].rearrange("p (n j) -> p n j", j=4), in_=w2_raw[:].rearrange("p j n -> p n j"))
                 nc.vector.tensor_copy(out=b2_f[:], in_=b2_raw[:, 0:1])
                 nc.vector.quantize_mx(out=w2_q[:].bitcast(FP8X4), scales=w2_s[:], in_=w2_g[:])
-            cast_s(i + 2)
-            turn_f(i)
+            turn_o(i - 3)
+            clamp_b(i - 5)
             quant_h(i - 2)
-            clamp_a(i - 3)
-            quant_x(i)
-            weave(i - 1)
-            mm1(i, (0, 1))
             mm2(i - 2)
-            copy_f(i)
+            cast_s(i + 2)
+            quant_x(i)
             unturn(i + 1, 0)
-            clamp_b(i - 3)
-            unturn(i + 1, 1)
+            mm1(i, (0, 1))
+            mul_f(i - 3)
+            finish(i - 6)
+            weave(i - 1)
+            squares(i - 4)
+            add_b2(i - 2)
             relu(i, (0, 1))
+            clamp_a(i - 4)
             mm1(i, (2, 3))
-            message(i - 2)
-            finish(i - 3)
-            relu(i, (2, 3))
             turn(i + 2, 0)
-            turn_m(i - 2)
-            turn(i + 2, 1)

from contextlib import ExitStack

import concourse.mybir as mybir
from concourse.masks import make_identity

E, K, H, N = 16384, 512, 512, 128
P = 128
TOK = 512
J = TOK // P
STEPS = E // TOK
FLOPS = 2 * E * H * (K + N)
LAST = 32

F32 = mybir.dt.float32
BF16 = mybir.dt.bfloat16
U32 = mybir.dt.uint32
U8 = mybir.dt.uint8
FP8 = mybir.dt.float8_e4m3fn
FP8X4 = mybir.dt.float8_e4m3fn_x4
ACT = mybir.ActivationFunctionType
ALU = mybir.AluOpType


def tile_filter_pa_t_kernel(tc, x_bytes, x_scale, f_weights, w1, node_bias, w2, b2, out):
    nc = tc.nc
    x_view = x_bytes.rearrange("(g p j) k -> g p (j k)", p=P, j=J)
    f_view = f_weights.rearrange("(g p j) n -> g p (j n)", p=P, j=J)
    o_view = out.rearrange("(g p j) n -> g p (j n)", p=P, j=J)

    with ExitStack() as ctx:
        const = ctx.enter_context(tc.tile_pool(name="const", bufs=1))
        load = ctx.enter_context(tc.tile_pool(name="load", bufs=6))
        fload = ctx.enter_context(tc.tile_pool(name="fload", bufs=9))
        one = ctx.enter_context(tc.tile_pool(name="one", bufs=1))
        work = ctx.enter_context(tc.tile_pool(name="work", bufs=3))
        tail = ctx.enter_context(tc.tile_pool(name="tail", bufs=8))
        xt_pool = ctx.enter_context(tc.psum_pool(name="xt_pool", bufs=2))
        h_pool = ctx.enter_context(tc.psum_pool(name="h_pool", bufs=3))
        o_pool = ctx.enter_context(tc.psum_pool(name="o_pool", bufs=1))
        m_pool = ctx.enter_context(tc.psum_pool(name="m_pool", bufs=2))
        ctx.enter_context(tc.manual_schedule())

        xb, fb = {}, {}

        def fetch(g):
            if not 0 <= g < STEPS:
                return
            xb[g] = load.tile([P, J * K], U8, name="xb_t", align_bytes=64)
            nc.sync.dma_start(out=xb[g][:], in_=x_view[g])

        def fetch_f(g):
            if not 0 <= g < STEPS:
                return
            fb[g] = fload.tile([P, J * N], BF16, name="fb_t", align_bytes=64)
            nc.sync.dma_start(out=fb[g][:], in_=f_view[g])

        fetch(0)
        sc = const.tile([P, 4], F32, name="sc", align_bytes=64)
        nc.sync.dma_start(out=sc[:], in_=x_scale.rearrange("o (p t) -> p (o t)", t=4))
        w1_raw = const.tile([P, 4, H], BF16, name="w1_raw", align_bytes=64)
        nc.sync.dma_start(out=w1_raw[:], in_=w1.rearrange("(p j) c -> p j c", j=4))
        fetch(1)
        nb_raw = const.tile([P, 4], BF16, name="nb_raw")
        nc.sync.dma_start(out=nb_raw[:], in_=node_bias.rearrange("(p t) -> p t", t=4))
        w2_raw = const.tile([P, 4, N], BF16, name="w2_raw", align_bytes=64)
        nc.sync.dma_start(out=w2_raw[:], in_=w2.rearrange("(p j) n -> p j n", j=4))
        b2_raw = const.tile([P, 2], BF16, name="b2_raw", align_bytes=64)
        nc.sync.dma_start(out=b2_raw[:, 0:1], in_=b2.rearrange("(p o) -> p o", o=1))
        fetch_f(0)
        fetch(2)
        fetch_f(1)
        fetch(3)
        fetch_f(2)

        ident = const.tile([P, P], F32, name="ident", align_bytes=64)
        make_identity(nc, ident[:])

        warm = const.tile([P, 1], F32, name="warm")
        nc.vector.memset(warm[:], 1.0)
        minus_one = const.tile([P, 1], F32, name="minus_one")
        nc.vector.memset(minus_one[:], -1.0)
        warm2 = const.tile([P, 1], F32, name="warm2")
        nc.scalar.activation(out=warm2[:], in_=warm[:], func=ACT.Abs_reciprocal_sqrt)

        nbias = const.tile([P, 4], F32, name="nbias")
        w1_g = const.tile([P, 4 * H], BF16, name="w1_g", align_bytes=64)
        w1_q = const.tile([P, H], U32, name="w1_q", align_bytes=64)
        w1_s = const.tile([P, H], U8, name="w1_s", align_bytes=64)
        w2_g = const.tile([P, 4 * N], BF16, name="w2_g", align_bytes=64)
        w2_q = const.tile([P, N], U32, name="w2_q", align_bytes=64)
        w2_s = const.tile([P, N], U8, name="w2_s", align_bytes=64)
        b2_f = const.tile([P, 1], F32, name="b2_f")

        xw, xt, xg, xq, xs, ht, hp, hg, hq, hs, ot, m0, mp, mm, ss, nr, fac = ({} for _ in range(17))

        def ok(g):
            return 0 <= g < STEPS

        def vector_cols(g):
            if g == 0:
                return 1536
            if g == 1:
                return 0
            return 0 if g >= STEPS - 1 else 768

        def wide(g):
            if g not in xw:
                xw[g] = work.tile([P, J * K], BF16, name="xw_t", align_bytes=64)

        def cast_v(g):
            if ok(g):
                wide(g)
                c = vector_cols(g)
                if c:
                    nc.vector.tensor_copy(out=xw[g][:, :c], in_=xb[g][:, :c].bitcast(FP8))

        def cast_s(g):
            if ok(g):
                wide(g)
                c = vector_cols(g)
                if c < J * K:
                    nc.scalar.copy(out=xw[g][:, c:], in_=xb[g][:, c:].bitcast(FP8))

        def turn(g, b):
            if not ok(g):
                return
            words = xw[g][:].bitcast(F32)
            t = xt_pool.tile([P, 2, 2 * P], F32, name="xt_t")
            for jj in range(2):
                j = 2 * b + jj
                for u in range(2):
                    nc.tensor.transpose(t[:, u, jj * P : (jj + 1) * P], words[:, j * (K // 2) + u : (j + 1) * (K // 2) : 2], ident[:])
            xt[g, b] = t

        def unturn(g, b):
            if not ok(g):
                return
            if g not in xg:
                xg[g] = work.tile([P, TOK * 4], BF16, name="xg_t", align_bytes=64)
            nc.vector.tensor_tensor(
                out=xg[g][:, b * 1024 : (b + 1) * 1024].rearrange("p (r u e) -> p r u e", u=2, e=2),
                in0=xt[g, b][:].rearrange("p u r -> p (u r)").bitcast(BF16).rearrange("p (u r e) -> p r u e", u=2, e=2),
                in1=sc[:].rearrange("p (o u e) -> p o u e", o=1, u=2).to_broadcast([P, 2 * P, 2, 2]),
                op=ALU.mult,
            )

        def quant_x(g):
            if ok(g):
                xq[g] = work.tile([P, TOK], U32, name="xq_t", align_bytes=64)
                xs[g] = work.tile([P, TOK], U8, name="xs_t", align_bytes=64)
                nc.vector.quantize_mx(out=xq[g][:].bitcast(FP8X4), scales=xs[g][:], in_=xg[g][:])

        def mm1(g, ts):
            if not ok(g):
                return
            for t in ts:
                ht[g, t] = h_pool.tile([P, TOK], F32, name="h_t")
                nc.tensor.matmul_mx(out=ht[g, t][:], lhsT=w1_q[:, t * P : (t + 1) * P].bitcast(FP8X4), lhsT_scale=w1_s[:, t * P : (t + 1) * P], rhs=xq[g][:].bitcast(FP8X4), rhs_scale=xs[g][:], start=True, stop=True)

        def relu(g, ts):
            if not ok(g):
                return
            if g not in hp:
                hp[g] = work.tile([P, 4, TOK], BF16, name="hp_t", align_bytes=64)
            for t in ts:
                if g == STEPS - 1 and "SSSS"[t] == "V":
                    nc.vector.tensor_scalar(out=hp[g][:, t, :], in0=ht[g, t][:], scalar1=nbias[:, t : t + 1], scalar2=0.0, op0=ALU.add, op1=ALU.max)
                else:
                    nc.scalar.activation(out=hp[g][:, t, :], in_=ht[g, t][:], func=ACT.Relu, bias=nbias[:, t : t + 1])

        def weave_part(engine, g, c0, c1):
            d = hg[g][:, 4 * c0 : 4 * c1].rearrange("p (c i t) -> p c t i", i=4, t=4)
            s = hp[g][:, :, c0:c1].rearrange("p t (c i) -> p c t i", i=4)
            if engine == "gpsimd":
                nc.gpsimd.tensor_scalar(out=d, in0=s, scalar1=1.0, scalar2=0.0, op0=ALU.mult, op1=ALU.add)
            elif engine == "vector":
                nc.vector.tensor_copy(out=d, in_=s)
            else:
                nc.scalar.copy(out=d, in_=s)

        def weave(g):
            if not ok(g):
                return
            hg[g] = one.tile([P, TOK * 4], BF16, name="hg_t", align_bytes=64)
            if g >= LAST:
                weave_part("vector", g, 0, 512)
            else:
                for c in range(0, TOK, 512):
                    weave_part("gpsimd", g, c, c + 512)

        def quant_h(g):
            if ok(g):
                hq[g] = work.tile([P, TOK], U32, name="hq_t", align_bytes=64)
                hs[g] = work.tile([P, TOK], U8, name="hs_t", align_bytes=64)
                nc.vector.quantize_mx(out=hq[g][:].bitcast(FP8X4), scales=hs[g][:], in_=hg[g][:])

        def mm2(g):
            if ok(g):
                ot[g] = o_pool.tile([P, TOK], F32, name="o_t")
                nc.tensor.matmul_mx(out=ot[g][:], lhsT=w2_q[:].bitcast(FP8X4), lhsT_scale=w2_s[:], rhs=hq[g][:].bitcast(FP8X4), rhs_scale=hs[g][:], start=True, stop=True)

        def add_b2(g):
            if ok(g):
                m0[g] = work.tile([P, TOK], F32, name="m0_t", align_bytes=64)
                nc.vector.tensor_scalar(out=m0[g][:], in0=ot[g][:], scalar1=b2_f[:], scalar2=None, op0=ALU.add)

        def turn_o(g):
            if ok(g):
                mp[g] = m_pool.tile([P, J * N], F32, name="mp_t")
                for j in range(J):
                    nc.tensor.transpose(mp[g][:, j * N : (j + 1) * N], m0[g][:, j * P : (j + 1) * P], ident[:])

        def mul_f(g):
            if ok(g):
                mm[g] = tail.tile([P, J * N], F32, name="mm_t", align_bytes=64)
                nc.vector.tensor_tensor(out=mm[g][:], in0=mp[g][:], in1=fb[g][:], op=ALU.mult)

        def paired(g):
            return g < STEPS - 2

        def last_of_group(g):
            return g % 2 == 1 or not paired(g)

        def col(g):
            return J * (g % 2) if paired(g) else 0

        def width(g):
            return 2 * J if paired(g) else J

        def squares(g):
            if not ok(g):
                return
            if paired(g) and g % 2 == 1:
                ss[g] = ss[g - 1]
            else:
                ss[g] = tail.tile([P, 2 * J], F32, name="ss_t")
            junk = work.tile([P, N], F32, name="junk_t", align_bytes=64)
            for j in range(J):
                c = col(g) + j
                nc.scalar.activation(out=junk[:], in_=mm[g][:, j * N : (j + 1) * N], func=ACT.Square, accum_out=ss[g][:, c : c + 1])

        def clamp_a(g):
            if ok(g) and last_of_group(g):
                nr[g] = tail.tile([P, 2 * J], F32, name="nr_t")
                nc.scalar.activation(out=nr[g][:, : width(g)], in_=ss[g][:, : width(g)], func=ACT.Relu, bias=minus_one[:])

        def clamp_b(g):
            if ok(g) and last_of_group(g):
                fac[g] = tail.tile([P, 2 * J], F32, name="fac_t")
                nc.scalar.activation(out=fac[g][:, : width(g)], in_=nr[g][:, : width(g)], func=ACT.Abs_reciprocal_sqrt, bias=warm[:])
                if paired(g):
                    fac[g - 1] = fac[g]

        def finish(g):
            if not ok(g):
                return
            y = tail.tile([P, J * N], F32, name="y_t", align_bytes=64)
            for j in range(J):
                f = fac[g][:, col(g) + j : col(g) + j + 1]
                nc.scalar.activation(out=y[:, j * N : (j + 1) * N], in_=mm[g][:, j * N : (j + 1) * N], func=ACT.Copy, scale=f)
            nc.sync.dma_start(out=o_view[g], in_=y[:])

        nc.scalar.copy(out=nbias[:], in_=nb_raw[:])
        cast_s(0)
        cast_s(1)
        cast_v(1)
        cast_v(0)
        nc.vector.tensor_copy(out=w1_g[:].rearrange("p (t m j) -> p t m j", t=4, j=4), in_=w1_raw[:].rearrange("p j (m t) -> p t m j", t=4))
        turn(0, 1)
        unturn(0, 1)
        turn(0, 0)
        turn(1, 0)
        nc.vector.quantize_mx(out=w1_q[:].bitcast(FP8X4), scales=w1_s[:], in_=w1_g[:])
        unturn(0, 0)
        turn(1, 1)

        for i in range(STEPS + 6):
            fetch(i + 4)
            fetch_f(i + 3)
            if i > 0:
                unturn(i, 1)
            relu(i - 1, (2, 3))
            if i + 1 > 1:
                turn(i + 1, 1)
            cast_v(i + 2)
            if i == 0:
                nc.vector.tensor_copy(out=w2_g[:].rearrange("p (n j) -> p n j", j=4), in_=w2_raw[:].rearrange("p j n -> p n j"))
                nc.vector.tensor_copy(out=b2_f[:], in_=b2_raw[:, 0:1])
                nc.vector.quantize_mx(out=w2_q[:].bitcast(FP8X4), scales=w2_s[:], in_=w2_g[:])
            turn_o(i - 3)
            clamp_b(i - 5)
            quant_h(i - 2)
            mm2(i - 2)
            cast_s(i + 2)
            quant_x(i)
            unturn(i + 1, 0)
            mm1(i, (0, 1))
            mul_f(i - 3)
            finish(i - 6)
            weave(i - 1)
            squares(i - 4)
            add_b2(i - 2)
            relu(i, (0, 1))
            clamp_a(i - 4)
            mm1(i, (2, 3))
            turn(i + 2, 0)
